import numpy as np
import ml_dtypes


def mxq(x, axis, fmt="e4m3"):
    dtype, down = {"e4m3": (ml_dtypes.float8_e4m3fn, 7), "e5m2": (ml_dtypes.float8_e5m2, 14)}[fmt]
    v = np.moveaxis(np.asarray(x, np.float32).astype(ml_dtypes.bfloat16).astype(np.float64), axis, -1)
    blocks = v.reshape(v.shape[:-1] + (-1, 32))
    amax = np.abs(blocks).max(-1, keepdims=True)
    byte = np.maximum(np.where(amax > 0, np.frexp(amax)[1] - 1 + 127, 0) - down, 1)
    scale = np.exp2(byte - 127.0)
    codes = (blocks / scale).astype(np.float32).astype(dtype).astype(np.float64)
    return np.moveaxis((codes * scale).reshape(v.shape), -1, axis)


WIDE = False


def mx_kscale(k):
    if not WIDE:
        return np.ones(k)
    levels = np.array([10, -10, 5, -5, 0])
    a = np.random.permutation(np.resize(levels, k // 512 * 4)).reshape(k // 512, 4)
    idx = np.arange(k)
    return np.exp2(a[idx // 512, idx % 128 // 32])


BF16 = ml_dtypes.bfloat16


def bf(x):
    return np.asarray(x, np.float32).astype(BF16)


def f64(x):
    return np.asarray(x).astype(np.float64)


N, S, K, Yd, Xd = 4096, 4, 16, 512, 256
LOG_2PI = np.log(2.0 * np.pi)


def softplus(v):
    return np.maximum(v, 0.0) + np.log(1.0 + np.exp(-np.abs(v)))


def log_softmax(v, axis):
    m = v - v.max(axis, keepdims=True)
    return m - np.log(np.exp(m).sum(axis, keepdims=True))


def mv_gaussian_log_prob(value, mu, sig_diags, event_shape):
    diff = value - mu
    M = np.sum((diff / sig_diags) ** 2, axis=-1)
    half_log_det = np.sum(np.log(sig_diags), axis=-1)
    return -0.5 * (event_shape * LOG_2PI + M) - half_log_det


def setup_inputs():
    s = mx_kscale(Yd)
    return {"Y": bf(np.random.standard_normal((N, Yd)) * 0.5 * s),
            "We_mu": bf(np.random.standard_normal((Yd, Xd)) * 2.0 / np.sqrt(Yd) / s[:, None]),
            "be_mu": bf(np.random.standard_normal(Xd) * 0.1),
            "We_sig": bf(np.random.standard_normal((Yd, Xd)) * 1.0 / np.sqrt(Yd) / s[:, None]),
            "be_sig": bf(-3.0 + np.random.standard_normal(Xd) * 0.1),
            "phi_mus": bf(np.random.standard_normal((K, Xd)) * 3.0 / np.sqrt(Xd)),
            "phi_sigs": bf(1.0 + (np.random.random_sample((K, Xd)) - 0.5) * 9.0 / np.sqrt(Xd)),
            "phi_logits": bf(np.random.standard_normal(K))}


def reference(Y, We_mu, be_mu, We_sig, be_sig, phi_mus, phi_sigs, phi_logits):
    Yq = mxq(f64(Y), 1, "e4m3")
    enc_mu = (Yq @ mxq(f64(We_mu), 0, "e4m3")) + f64(be_mu)
    enc_sig = softplus((Yq @ mxq(f64(We_sig), 0, "e4m3")) + f64(be_sig)) + 1e-3
    log_pi = log_softmax(f64(phi_logits), -1)
    std_k = enc_sig[:, None, :] + f64(phi_sigs)[None, :, :]
    z_logits = log_pi[None, :] + mv_gaussian_log_prob(enc_mu[:, None, :], f64(phi_mus)[None, :, :], std_k, Xd)
    z_log_probs = log_softmax(z_logits, -1)
    return enc_mu, enc_sig, z_log_probs

@@ -1,0 +1,367 @@
+from contextlib import ExitStack
+
+import concourse.mybir as mybir
+from concourse.masks import make_identity
+
+F32 = mybir.dt.float32
+BF16 = mybir.dt.bfloat16
+U32 = mybir.dt.uint32
+U8 = mybir.dt.uint8
+FP8X4 = mybir.dt.float8_e4m3fn_x4
+ALU = mybir.AluOpType
+ACT = mybir.ActivationFunctionType
+AX = mybir.AxisListType
+
+P = 128
+N_ROWS = 4096
+K_IN = 512
+D = 256
+H = D // P
+KC = 16
+CHUNK = 512
+TPC = CHUNK // P
+N_CHUNKS = N_ROWS // CHUNK
+N_TILES = N_ROWS // P
+N_UNITS = N_CHUNKS * KC
+PACK = 4
+
+SIG_FLOOR = 0.001
+SOFTPLUS_LINEAR_FROM = 40.0
+
+ROW_PHI_MUS = 0
+ROW_PHI_SIGS = KC
+ROW_BE_MU = 2 * KC
+ROW_BE_SIG = 2 * KC + 1
+
+GPSIMD_EVERY = 4
+SUM_LEAD = 3
+REDUCE_LAG = 2
+
+FLOPS = 2 * N_ROWS * K_IN * 2 * D
+
+
+def tile_deepgmm_pa_t_kernel(
+    tc, Y, We_mu, be_mu, We_sig, be_sig, phi_mus, phi_sigs, phi_logits, out_0, out_1, out_2
+):
+    nc = tc.nc
+    y_view = Y.rearrange("(p t) k -> p (t k)", t=N_TILES)
+    mu_view = out_0.rearrange("(p t) d -> p t d", t=N_TILES)
+    sig_view = out_1.rearrange("(p t) d -> p t d", t=N_TILES)
+    z_view = out_2.rearrange("(p t) k -> p (t k)", t=N_TILES)
+
+    with ExitStack() as ctx:
+        ctx.enter_context(tc.manual_schedule())
+        keep = ctx.enter_context(tc.tile_pool(name="keep", bufs=1))
+
+        ident = keep.tile([P, P], F32, name="ident")
+        w_codes = keep.tile([P, 2 * D], U32, name="w_codes", align_bytes=64)
+        w_scales = keep.tile([P, 2 * D], U8, name="w_scales", align_bytes=64)
+        y_codes = keep.tile([P, N_ROWS], U32, name="y_codes", align_bytes=64)
+        y_scales = keep.tile([P, N_ROWS], U8, name="y_scales", align_bytes=64)
+        par = keep.tile([P, H, P], F32, name="par")
+        mu_shift = keep.tile([P, H, KC], F32, name="mu_shift")
+        sig_shift = keep.tile([P, H, KC], F32, name="sig_shift")
+        be_mu_rows = keep.tile([P, D], F32, name="be_mu_rows")
+        logit_rows = keep.tile([P, KC], F32, name="logit_rows")
+        one = keep.tile([P, 1], F32, name="one")
+        half = keep.tile([P, 1], F32, name="half")
+        ln_half = keep.tile([P, 1], F32, name="ln_half")
+        half_ln_half = keep.tile([P, 1], F32, name="half_ln_half")
+        sig_t = keep.tile([P, N_CHUNKS, H, CHUNK], F32, name="sig_t")
+        energy = keep.tile([P, KC, N_TILES], F32, name="energy")
+
+        def d_layout_sums(pool, c, first_block):
+            rows = slice(c * CHUNK, (c + 1) * CHUNK)
+            sums = []
+            for h in range(H):
+                cols = slice((first_block + h) * P, (first_block + h + 1) * P)
+                d_sum = pool.tile([P, CHUNK], F32, name="d_sum", tag="d_sum")
+                nc.tensor.matmul_mx(
+                    out=d_sum[:],
+                    lhsT=w_codes[:, cols].bitcast(FP8X4),
+                    lhsT_scale=w_scales[:, cols],
+                    rhs=y_codes[:, rows].bitcast(FP8X4),
+                    rhs_scale=y_scales[:, rows],
+                    start=True,
+                    stop=True,
+                )
+                sums.append(d_sum)
+            return sums
+
+        with ExitStack() as first:
+            once = first.enter_context(tc.tile_pool(name="once", bufs=1))
+            raw_pool = first.enter_context(tc.tile_pool(name="raw", bufs=N_CHUNKS))
+            stage = first.enter_context(tc.tile_pool(name="stage", bufs=2))
+            psum_a = first.enter_context(tc.psum_pool(name="psum_a", bufs=2))
+
+            make_identity(nc, ident[:])
+
+            rows_bf = once.tile([P, D], BF16, name="rows_bf")
+            nc.vector.memset(rows_bf[:], 0.0)
+            nc.scalar.dma_start(out=rows_bf[ROW_PHI_MUS : ROW_PHI_MUS + KC, :], in_=phi_mus)
+            nc.scalar.dma_start(out=rows_bf[ROW_PHI_SIGS : ROW_PHI_SIGS + KC, :], in_=phi_sigs)
+            nc.scalar.dma_start(out=rows_bf[ROW_BE_MU : ROW_BE_MU + 1, :], in_=be_mu.rearrange("(o d) -> o d", o=1))
+            nc.scalar.dma_start(out=rows_bf[ROW_BE_SIG : ROW_BE_SIG + 1, :], in_=be_sig.rearrange("(o d) -> o d", o=1))
+            be_mu_bf = once.tile([P, D], BF16, name="be_mu_bf")
+            nc.scalar.dma_start(out=be_mu_bf[:], in_=be_mu.partition_broadcast(P))
+            logit_bf = once.tile([P, KC], BF16, name="logit_bf")
+            nc.scalar.dma_start(out=logit_bf[:], in_=phi_logits.partition_broadcast(P))
+
+            nc.vector.memset(one[:], 1.0)
+            nc.vector.memset(half[:], 0.5)
+            nc.scalar.activation(out=ln_half[:], in_=half[:], func=ACT.Ln)
+
+            y_raw = []
+            w_raw = once.tile([P, PACK, 2 * D], BF16, name="w_raw")
+            for c in range(N_CHUNKS):
+                y_chunk = raw_pool.tile([P, TPC * K_IN], BF16, name="y_chunk")
+                nc.sync.dma_start(out=y_chunk[:], in_=y_view[:, c * TPC * K_IN : (c + 1) * TPC * K_IN])
+                y_raw.append(y_chunk)
+                if c == 0:
+                    for m, weight in enumerate((We_mu, We_sig)):
+                        for u in range(2):
+                            nc.sync.dma_start(
+                                out=w_raw[:, 2 * u : 2 * u + 2, m * D : (m + 1) * D],
+                                in_=weight[u * 2 * P : (u + 1) * 2 * P, :].rearrange("(q e) c -> q e c", e=2),
+                            )
+
+            def transpose_y(c):
+                y_grp = stage.tile([P, PACK * CHUNK], BF16, name="y_grp", align_bytes=64)
+                words = y_raw[c][:].bitcast(F32)
+                grp_words = y_grp[:].bitcast(F32)
+                for pair in range(TPC // 2):
+                    y_t = psum_a.tile([P, 2, 2 * P], F32, name="y_t")
+                    for i in range(2):
+                        first_word = (2 * pair + i) * (K_IN // 2)
+                        for u in range(2):
+                            nc.tensor.transpose(
+                                y_t[:, u, i * P : (i + 1) * P],
+                                words[:, first_word + u * P : first_word + (u + 1) * P],
+                                ident[:],
+                            )
+                    nc.scalar.copy(
+                        out=grp_words[:, pair * 4 * P : (pair + 1) * 4 * P].rearrange("p (n u) -> p n u", u=2),
+                        in_=y_t[:].rearrange("p u n -> p n u"),
+                    )
+                return y_grp
+
+            y_grp_next = transpose_y(0)
+
+            w_grp = once.tile([P, 2 * D, PACK], BF16, name="w_grp", align_bytes=64)
+            nc.vector.tensor_copy(out=w_grp[:], in_=w_raw[:].rearrange("p t c -> p c t"))
+            rows_f32 = once.tile([P, D], F32, name="rows_f32")
+            nc.vector.tensor_copy(out=rows_f32[:], in_=rows_bf[:])
+            nc.vector.quantize_mx(
+                out=w_codes[:].bitcast(FP8X4), scales=w_scales[:], in_=w_grp[:].rearrange("p c t -> p (c t)")
+            )
+            par_ps = psum_a.tile([P, H, P], F32, name="par_ps", tag="y_t")
+            for h in range(H):
+                nc.tensor.transpose(par_ps[:, h, :], rows_f32[:, h * P : (h + 1) * P], ident[:])
+            nc.vector.tensor_copy(out=par[:], in_=par_ps[:])
+            nc.vector.tensor_copy(out=be_mu_rows[:], in_=be_mu_bf[:])
+            nc.vector.tensor_copy(out=logit_rows[:], in_=logit_bf[:])
+            nc.vector.tensor_scalar(out=half_ln_half[:], in0=ln_half[:], scalar1=0.5, scalar2=None, op0=ALU.mult)
+            for h in range(H):
+                nc.vector.tensor_scalar(
+                    out=mu_shift[:, h, :],
+                    in0=par[:, h, ROW_PHI_MUS : ROW_PHI_MUS + KC],
+                    scalar1=par[:, h, ROW_BE_MU : ROW_BE_MU + 1],
+                    scalar2=None,
+                    op0=ALU.subtract,
+                )
+            nc.vector.tensor_scalar(
+                out=sig_shift[:],
+                in0=par[:, :, ROW_PHI_SIGS : ROW_PHI_SIGS + KC],
+                scalar1=SIG_FLOOR,
+                scalar2=None,
+                op0=ALU.add,
+            )
+
+            for c in range(N_CHUNKS):
+                y_grp = y_grp_next
+                if c + 1 < N_CHUNKS:
+                    y_grp_next = transpose_y(c + 1)
+                rows = slice(c * CHUNK, (c + 1) * CHUNK)
+                nc.vector.quantize_mx(out=y_codes[:, rows].bitcast(FP8X4), scales=y_scales[:, rows], in_=y_grp[:])
+
+                sig_sums = d_layout_sums(psum_a, c, H)
+                for h in range(H):
+                    nc.vector.tensor_scalar(
+                        out=sig_t[:, c, h, :],
+                        in0=sig_sums[h][:],
+                        scalar1=par[:, h, ROW_BE_SIG : ROW_BE_SIG + 1],
+                        scalar2=SOFTPLUS_LINEAR_FROM,
+                        op0=ALU.add,
+                        op1=ALU.min,
+                    )
+                nc.scalar.activation(out=sig_t[:, c, :, :], in_=sig_t[:, c, :, :], func=ACT.Exp)
+
+                mu_out = stage.tile([P, TPC, D], F32, name="mu_out")
+                for pair in range(TPC // 2):
+                    mu_n = psum_a.tile([P, 2, D], F32, name="mu_n")
+                    for i in range(2):
+                        cols = slice(c * CHUNK + (2 * pair + i) * P, c * CHUNK + (2 * pair + i + 1) * P)
+                        nc.tensor.matmul_mx(
+                            out=mu_n[:, i, :],
+                            lhsT=y_codes[:, cols].bitcast(FP8X4),
+                            lhsT_scale=y_scales[:, cols],
+                            rhs=w_codes[:, 0:D].bitcast(FP8X4),
+                            rhs_scale=w_scales[:, 0:D],
+                            start=True,
+                            stop=True,
+                        )
+                    nc.vector.tensor_tensor(
+                        out=mu_out[:, 2 * pair : 2 * pair + 2, :],
+                        in0=mu_n[:],
+                        in1=be_mu_rows[:].unsqueeze(1).to_broadcast([P, 2, D]),
+                        op=ALU.add,
+                    )
+                nc.sync.dma_start(out=mu_view[:, c * TPC : (c + 1) * TPC, :], in_=mu_out[:])
+
+        log_pool = ctx.enter_context(tc.tile_pool(name="logs", bufs=KC + 2))
+        sum_pool = ctx.enter_context(tc.tile_pool(name="log_sums", bufs=SUM_LEAD + 3))
+        wgt_pool = ctx.enter_context(tc.tile_pool(name="wgts", bufs=12))
+        out_pool = ctx.enter_context(tc.tile_pool(name="outs", bufs=2))
+        psum = ctx.enter_context(tc.psum_pool(name="psum", bufs=4))
+
+        for c in range(N_CHUNKS + 1):
+            if c < N_CHUNKS:
+                nc.scalar.activation(out=sig_t[:, c, :, :], in_=sig_t[:, c, :, :], func=ACT.Ln, bias=one[:])
+                sig_sums = d_layout_sums(psum, c, H)
+                for h in range(H):
+                    nc.vector.scalar_tensor_tensor(
+                        out=sig_t[:, c, h, :],
+                        in0=sig_sums[h][:],
+                        scalar=par[:, h, ROW_BE_SIG : ROW_BE_SIG + 1],
+                        in1=sig_t[:, c, h, :],
+                        op0=ALU.add,
+                        op1=ALU.max,
+                    )
+            if c > 0:
+                b = c - 1
+                sig_out = out_pool.tile([P, TPC, D], F32, name="sig_out")
+                for pair in range(TPC // 2):
+                    sig_n = psum.tile([P, 2, D], F32, name="sig_n", tag="acc")
+                    for i in range(2):
+                        cols = slice((2 * pair + i) * P, (2 * pair + i + 1) * P)
+                        for h in range(H):
+                            nc.tensor.transpose(sig_n[:, i, h * P : (h + 1) * P], sig_t[:, b, h, cols], ident[:])
+                    nc.vector.tensor_scalar(
+                        out=sig_out[:, 2 * pair : 2 * pair + 2, :],
+                        in0=sig_n[:],
+                        scalar1=SIG_FLOOR,
+                        scalar2=None,
+                        op0=ALU.add,
+                    )
+                nc.sync.dma_start(out=sig_view[:, b * TPC : (b + 1) * TPC, :], in_=sig_out[:])
+
+        logs = {}
+        wgts = {}
+        log_sums = {}
+        accs = {}
+        mu_sums = {}
+
+        def gpsimd_squares(j):
+            return j % GPSIMD_EVERY == GPSIMD_EVERY - 1
+
+        def take_logs(c):
+            for k in range(KC):
+                unit_logs = log_pool.tile([P, H, CHUNK], F32, name="unit_logs")
+                for h in range(H):
+                    nc.scalar.activation(
+                        out=unit_logs[:, h, :], in_=sig_t[:, c, h, :], func=ACT.Ln, bias=sig_shift[:, h, k : k + 1]
+                    )
+                logs[c * KC + k] = unit_logs
+
+        def take_weights(c):
+            for j in range(c * KC, (c + 1) * KC):
+                wgt = wgt_pool.tile([P, H, CHUNK], F32, name="wgt")
+                if gpsimd_squares(j):
+                    nc.scalar.activation(out=wgt[:], in_=logs[j][:], func=ACT.Exp, bias=half_ln_half[:], scale=-1.0)
+                else:
+                    nc.scalar.activation(out=wgt[:], in_=logs[j][:], func=ACT.Exp, bias=ln_half[:], scale=-2.0)
+                wgts[j] = wgt
+
+        def add_logs(j):
+            log_sum = sum_pool.tile([P, CHUNK], F32, name="log_sum")
+            nc.gpsimd.tensor_tensor(out=log_sum[:], in0=logs[j][:, 0, :], in1=logs[j][:, 1, :], op=ALU.add)
+            log_sums[j] = log_sum
+
+        def weighted_squares(j):
+            c, k = divmod(j, KC)
+            wgt = wgts[j]
+            for step in range(1 if gpsimd_squares(j) else 2):
+                for h in range(H):
+                    nc.vector.scalar_tensor_tensor(
+                        out=wgt[:, h, :],
+                        in0=mu_sums[c][h][:],
+                        scalar=mu_shift[:, h, k : k + 1],
+                        in1=wgt[:, h, :],
+                        op0=ALU.subtract,
+                        op1=ALU.mult,
+                    )
+            if gpsimd_squares(j):
+                nc.gpsimd.tensor_tensor(out=wgt[:], in0=wgt[:], in1=wgt[:], op=ALU.mult)
+
+        def add_over_halves(j):
+            acc = psum.tile([P, TPC, P], F32, name="acc", tag="acc")
+            for t in range(TPC):
+                cols = slice(t * P, (t + 1) * P)
+                parts = (log_sums[j][:, cols], wgts[j][:, 0, cols], wgts[j][:, 1, cols])
+                for i, part in enumerate(parts):
+                    nc.tensor.matmul(
+                        out=acc[:, t, :],
+                        lhsT=part,
+                        rhs=ident[:],
+                        is_transpose=True,
+                        start=(i == 0),
+                        stop=(i == len(parts) - 1),
+                    )
+            accs[j] = acc
+
+        def reduce_unit(j):
+            c, k = divmod(j, KC)
+            nc.vector.tensor_reduce(out=energy[:, k, c * TPC : (c + 1) * TPC], in_=accs[j][:], axis=AX.X, op=ALU.add)
+
+        mu_sums[0] = d_layout_sums(psum, 0, 0)
+        take_logs(0)
+        take_weights(0)
+        for j in range(SUM_LEAD):
+            add_logs(j)
+        for c in range(N_CHUNKS):
+            if c + 1 < N_CHUNKS:
+                mu_sums[c + 1] = d_layout_sums(psum, c + 1, 0)
+                take_logs(c + 1)
+            for j in range(c * KC, (c + 1) * KC):
+                if j + SUM_LEAD < N_UNITS:
+                    add_logs(j + SUM_LEAD)
+                weighted_squares(j)
+                add_over_halves(j)
+                if j >= REDUCE_LAG:
+                    reduce_unit(j - REDUCE_LAG)
+            if c + 1 < N_CHUNKS:
+                take_weights(c + 1)
+        for j in range(N_UNITS - REDUCE_LAG, N_UNITS):
+            reduce_unit(j)
+
+        z = out_pool.tile([P, N_TILES, KC], F32, name="z")
+        z_max = out_pool.tile([P, N_TILES], F32, name="z_max")
+        z_exp = out_pool.tile([P, N_TILES, KC], F32, name="z_exp")
+        z_sum = out_pool.tile([P, N_TILES], F32, name="z_sum")
+        nc.vector.tensor_tensor(
+            out=z[:],
+            in0=logit_rows[:].unsqueeze(1).to_broadcast([P, N_TILES, KC]),
+            in1=energy[:].rearrange("p k t -> p t k"),
+            op=ALU.subtract,
+        )
+        nc.vector.tensor_reduce(out=z_max[:], in_=z[:], axis=AX.X, op=ALU.max)
+        nc.vector.tensor_tensor(
+            out=z[:], in0=z[:], in1=z_max[:].unsqueeze(2).to_broadcast([P, N_TILES, KC]), op=ALU.subtract
+        )
+        nc.scalar.activation(out=z_exp[:], in_=z[:], func=ACT.Exp)
+        nc.vector.tensor_reduce(out=z_sum[:], in_=z_exp[:], axis=AX.X, op=ALU.add)
+        nc.scalar.activation(out=z_sum[:], in_=z_sum[:], func=ACT.Ln)
+        nc.vector.tensor_tensor(
+            out=z[:], in0=z[:], in1=z_sum[:].unsqueeze(2).to_broadcast([P, N_TILES, KC]), op=ALU.subtract
+        )
+        nc.sync.dma_start(out=z_view, in_=z[:].rearrange("p t k -> p (t k)"))

@@ -33,9 +33,11 @@ ROW_PHI_SIGS = KC
 ROW_BE_MU = 2 * KC
 ROW_BE_SIG = 2 * KC + 1
 
-GPSIMD_EVERY = 4
+GPSIMD_EVERY = 3
 SUM_LEAD = 3
-REDUCE_LAG = 2
+REDUCE_LAG = 3
+NEXT_CHUNK_AT = 10
+BIG_SLOTS = KC
 
 FLOPS = 2 * N_ROWS * K_IN * 2 * D
 
@@ -70,12 +72,18 @@ def tile_deepgmm_pa_t_kernel(
         sig_t = keep.tile([P, N_CHUNKS, H, CHUNK], F32, name="sig_t")
         energy = keep.tile([P, KC, N_TILES], F32, name="energy")
 
-        def d_layout_sums(pool, c, first_block):
+        log_pool = ctx.enter_context(tc.tile_pool(name="logs", bufs=KC + 2))
+        sum_pool = ctx.enter_context(tc.tile_pool(name="log_sums", bufs=SUM_LEAD + 3))
+        big_pool = ctx.enter_context(tc.tile_pool(name="big", bufs=BIG_SLOTS))
+        out_pool = ctx.enter_context(tc.tile_pool(name="outs", bufs=3))
+        psum = ctx.enter_context(tc.psum_pool(name="psum", bufs=4))
+
+        def d_layout_sums(c, first_block):
             rows = slice(c * CHUNK, (c + 1) * CHUNK)
             sums = []
             for h in range(H):
                 cols = slice((first_block + h) * P, (first_block + h + 1) * P)
-                d_sum = pool.tile([P, CHUNK], F32, name="d_sum", tag="d_sum")
+                d_sum = psum.tile([P, CHUNK], F32, name="d_sum", tag="d_sum")
                 nc.tensor.matmul_mx(
                     out=d_sum[:],
                     lhsT=w_codes[:, cols].bitcast(FP8X4),
@@ -88,172 +96,171 @@ def tile_deepgmm_pa_t_kernel(
                 sums.append(d_sum)
             return sums
 
-        with ExitStack() as first:
-            once = first.enter_context(tc.tile_pool(name="once", bufs=1))
-            raw_pool = first.enter_context(tc.tile_pool(name="raw", bufs=N_CHUNKS))
-            stage = first.enter_context(tc.tile_pool(name="stage", bufs=2))
-            psum_a = first.enter_context(tc.psum_pool(name="psum_a", bufs=2))
+        make_identity(nc, ident[:])
 
-            make_identity(nc, ident[:])
+        rows_bf = keep.tile([P, D], BF16, name="rows_bf")
+        nc.vector.memset(rows_bf[:], 0.0)
+        nc.scalar.dma_start(out=rows_bf[ROW_PHI_MUS : ROW_PHI_MUS + KC, :], in_=phi_mus)
+        nc.scalar.dma_start(out=rows_bf[ROW_PHI_SIGS : ROW_PHI_SIGS + KC, :], in_=phi_sigs)
+        nc.scalar.dma_start(out=rows_bf[ROW_BE_MU : ROW_BE_MU + 1, :], in_=be_mu.rearrange("(o d) -> o d", o=1))
+        nc.scalar.dma_start(out=rows_bf[ROW_BE_SIG : ROW_BE_SIG + 1, :], in_=be_sig.rearrange("(o d) -> o d", o=1))
+        be_mu_bf = keep.tile([P, D], BF16, name="be_mu_bf")
+        nc.scalar.dma_start(out=be_mu_bf[:], in_=be_mu.partition_broadcast(P))
+        logit_bf = keep.tile([P, KC], BF16, name="logit_bf")
+        nc.scalar.dma_start(out=logit_bf[:], in_=phi_logits.partition_broadcast(P))
+        nc.vector.memset(one[:], 1.0)
+        nc.vector.memset(half[:], 0.5)
 
-            rows_bf = once.tile([P, D], BF16, name="rows_bf")
-            nc.vector.memset(rows_bf[:], 0.0)
-            nc.scalar.dma_start(out=rows_bf[ROW_PHI_MUS : ROW_PHI_MUS + KC, :], in_=phi_mus)
-            nc.scalar.dma_start(out=rows_bf[ROW_PHI_SIGS : ROW_PHI_SIGS + KC, :], in_=phi_sigs)
-            nc.scalar.dma_start(out=rows_bf[ROW_BE_MU : ROW_BE_MU + 1, :], in_=be_mu.rearrange("(o d) -> o d", o=1))
-            nc.scalar.dma_start(out=rows_bf[ROW_BE_SIG : ROW_BE_SIG + 1, :], in_=be_sig.rearrange("(o d) -> o d", o=1))
-            be_mu_bf = once.tile([P, D], BF16, name="be_mu_bf")
-            nc.scalar.dma_start(out=be_mu_bf[:], in_=be_mu.partition_broadcast(P))
-            logit_bf = once.tile([P, KC], BF16, name="logit_bf")
-            nc.scalar.dma_start(out=logit_bf[:], in_=phi_logits.partition_broadcast(P))
+        y_raw = []
+        w_raw = big_pool.tile([P, PACK, 2 * D], BF16, name="w_raw", tag="big", align_bytes=64)
+        for c in range(N_CHUNKS):
+            y_chunk = big_pool.tile([P, TPC * K_IN], BF16, name="y_chunk", tag="big", align_bytes=64)
+            nc.sync.dma_start(out=y_chunk[:], in_=y_view[:, c * TPC * K_IN : (c + 1) * TPC * K_IN])
+            y_raw.append(y_chunk)
+            if c == 0:
+                for m, weight in enumerate((We_mu, We_sig)):
+                    for u in range(2):
+                        nc.sync.dma_start(
+                            out=w_raw[:, 2 * u : 2 * u + 2, m * D : (m + 1) * D],
+                            in_=weight[u * 2 * P : (u + 1) * 2 * P, :].rearrange("(q e) c -> q e c", e=2),
+                        )
 
-            nc.vector.memset(one[:], 1.0)
-            nc.vector.memset(half[:], 0.5)
-            nc.scalar.activation(out=ln_half[:], in_=half[:], func=ACT.Ln)
+        y_banks = {}
+        y_grps = {}
 
-            y_raw = []
-            w_raw = once.tile([P, PACK, 2 * D], BF16, name="w_raw")
-            for c in range(N_CHUNKS):
-                y_chunk = raw_pool.tile([P, TPC * K_IN], BF16, name="y_chunk")
-                nc.sync.dma_start(out=y_chunk[:], in_=y_view[:, c * TPC * K_IN : (c + 1) * TPC * K_IN])
-                y_raw.append(y_chunk)
-                if c == 0:
-                    for m, weight in enumerate((We_mu, We_sig)):
-                        for u in range(2):
-                            nc.sync.dma_start(
-                                out=w_raw[:, 2 * u : 2 * u + 2, m * D : (m + 1) * D],
-                                in_=weight[u * 2 * P : (u + 1) * 2 * P, :].rearrange("(q e) c -> q e c", e=2),
-                            )
+        def transpose_y(c):
+            words = y_raw[c][:].bitcast(F32)
+            y_banks[c] = []
+            for pair in range(TPC // 2):
+                y_t = psum.tile([P, 2, 2 * P], F32, name="y_t", tag="acc")
+                for i in range(2):
+                    first_word = (2 * pair + i) * (K_IN // 2)
+                    for u in range(2):
+                        nc.tensor.transpose(
+                            y_t[:, u, i * P : (i + 1) * P],
+                            words[:, first_word + u * P : first_word + (u + 1) * P],
+                            ident[:],
+                        )
+                y_banks[c].append(y_t)
 
-            def transpose_y(c):
-                y_grp = stage.tile([P, PACK * CHUNK], BF16, name="y_grp", align_bytes=64)
-                words = y_raw[c][:].bitcast(F32)
-                grp_words = y_grp[:].bitcast(F32)
-                for pair in range(TPC // 2):
-                    y_t = psum_a.tile([P, 2, 2 * P], F32, name="y_t")
-                    for i in range(2):
-                        first_word = (2 * pair + i) * (K_IN // 2)
-                        for u in range(2):
-                            nc.tensor.transpose(
-                                y_t[:, u, i * P : (i + 1) * P],
-                                words[:, first_word + u * P : first_word + (u + 1) * P],
-                                ident[:],
-                            )
-                    nc.scalar.copy(
-                        out=grp_words[:, pair * 4 * P : (pair + 1) * 4 * P].rearrange("p (n u) -> p n u", u=2),
-                        in_=y_t[:].rearrange("p u n -> p n u"),
-                    )
-                return y_grp
+        def regroup_y(c):
+            y_grp = big_pool.tile([P, PACK * CHUNK], BF16, name="y_grp", tag="big", align_bytes=64)
+            grp_words = y_grp[:].bitcast(F32)
+            for pair in range(TPC // 2):
+                nc.vector.tensor_copy(
+                    out=grp_words[:, pair * 4 * P : (pair + 1) * 4 * P].rearrange("p (n u) -> p n u", u=2),
+                    in_=y_banks[c][pair][:].rearrange("p u n -> p n u"),
+                )
+            y_grps[c] = y_grp
 
-            y_grp_next = transpose_y(0)
+        transpose_y(0)
+        regroup_y(0)
 
-            w_grp = once.tile([P, 2 * D, PACK], BF16, name="w_grp", align_bytes=64)
-            nc.vector.tensor_copy(out=w_grp[:], in_=w_raw[:].rearrange("p t c -> p c t"))
-            rows_f32 = once.tile([P, D], F32, name="rows_f32")
-            nc.vector.tensor_copy(out=rows_f32[:], in_=rows_bf[:])
-            nc.vector.quantize_mx(
-                out=w_codes[:].bitcast(FP8X4), scales=w_scales[:], in_=w_grp[:].rearrange("p c t -> p (c t)")
+        w_grp = big_pool.tile([P, 2 * D, PACK], BF16, name="w_grp", tag="big", align_bytes=64)
+        nc.vector.tensor_copy(out=w_grp[:], in_=w_raw[:].rearrange("p t c -> p c t"))
+        rows_f32 = keep.tile([P, D], F32, name="rows_f32")
+        nc.vector.tensor_copy(out=rows_f32[:], in_=rows_bf[:])
+        nc.vector.quantize_mx(
+            out=w_codes[:].bitcast(FP8X4), scales=w_scales[:], in_=w_grp[:].rearrange("p c t -> p (c t)")
+        )
+        par_ps = psum.tile([P, H, P], F32, name="par_ps", tag="acc")
+        for h in range(H):
+            nc.tensor.transpose(par_ps[:, h, :], rows_f32[:, h * P : (h + 1) * P], ident[:])
+        nc.vector.tensor_copy(out=par[:], in_=par_ps[:])
+        nc.vector.tensor_copy(out=be_mu_rows[:], in_=be_mu_bf[:])
+        nc.vector.tensor_copy(out=logit_rows[:], in_=logit_bf[:])
+        for h in range(H):
+            nc.vector.tensor_scalar(
+                out=mu_shift[:, h, :],
+                in0=par[:, h, ROW_PHI_MUS : ROW_PHI_MUS + KC],
+                scalar1=par[:, h, ROW_BE_MU : ROW_BE_MU + 1],
+                scalar2=None,
+                op0=ALU.subtract,
             )
-            par_ps = psum_a.tile([P, H, P], F32, name="par_ps", tag="y_t")
-            for h in range(H):
-                nc.tensor.transpose(par_ps[:, h, :], rows_f32[:, h * P : (h + 1) * P], ident[:])
-            nc.vector.tensor_copy(out=par[:], in_=par_ps[:])
-            nc.vector.tensor_copy(out=be_mu_rows[:], in_=be_mu_bf[:])
-            nc.vector.tensor_copy(out=logit_rows[:], in_=logit_bf[:])
-            nc.vector.tensor_scalar(out=half_ln_half[:], in0=ln_half[:], scalar1=0.5, scalar2=None, op0=ALU.mult)
+        nc.vector.tensor_scalar(
+            out=sig_shift[:],
+            in0=par[:, :, ROW_PHI_SIGS : ROW_PHI_SIGS + KC],
+            scalar1=SIG_FLOOR,
+            scalar2=None,
+            op0=ALU.add,
+        )
+
+        def prepare(c):
+            if c + 1 < N_CHUNKS:
+                transpose_y(c + 1)
+            rows = slice(c * CHUNK, (c + 1) * CHUNK)
+            nc.vector.quantize_mx(out=y_codes[:, rows].bitcast(FP8X4), scales=y_scales[:, rows], in_=y_grps[c][:])
+            sig_sums = d_layout_sums(c, H)
+            mu_banks = []
+            for pair in range(TPC // 2):
+                mu_n = psum.tile([P, 2, D], F32, name="mu_n", tag="acc")
+                for i in range(2):
+                    cols = slice(c * CHUNK + (2 * pair + i) * P, c * CHUNK + (2 * pair + i + 1) * P)
+                    nc.tensor.matmul_mx(
+                        out=mu_n[:, i, :],
+                        lhsT=y_codes[:, cols].bitcast(FP8X4),
+                        lhsT_scale=y_scales[:, cols],
+                        rhs=w_codes[:, 0:D].bitcast(FP8X4),
+                        rhs_scale=w_scales[:, 0:D],
+                        start=True,
+                        stop=True,
+                    )
+                mu_banks.append(mu_n)
+            if c + 1 < N_CHUNKS:
+                regroup_y(c + 1)
             for h in range(H):
                 nc.vector.tensor_scalar(
-                    out=mu_shift[:, h, :],
-                    in0=par[:, h, ROW_PHI_MUS : ROW_PHI_MUS + KC],
-                    scalar1=par[:, h, ROW_BE_MU : ROW_BE_MU + 1],
-                    scalar2=None,
-                    op0=ALU.subtract,
+                    out=sig_t[:, c, h, :],
+                    in0=sig_sums[h][:],
+                    scalar1=par[:, h, ROW_BE_SIG : ROW_BE_SIG + 1],
+                    scalar2=SOFTPLUS_LINEAR_FROM,
+                    op0=ALU.add,
+                    op1=ALU.min,
                 )
-            nc.vector.tensor_scalar(
-                out=sig_shift[:],
-                in0=par[:, :, ROW_PHI_SIGS : ROW_PHI_SIGS + KC],
-                scalar1=SIG_FLOOR,
-                scalar2=None,
-                op0=ALU.add,
-            )
+            mu_out = out_pool.tile([P, TPC, D], F32, name="mu_out", tag="rows_out")
+            for pair in range(TPC // 2):
+                nc.vector.tensor_tensor(
+                    out=mu_out[:, 2 * pair : 2 * pair + 2, :],
+                    in0=mu_banks[pair][:],
+                    in1=be_mu_rows[:].unsqueeze(1).to_broadcast([P, 2, D]),
+                    op=ALU.add,
+                )
+            nc.sync.dma_start(out=mu_view[:, c * TPC : (c + 1) * TPC, :], in_=mu_out[:])
 
-            for c in range(N_CHUNKS):
-                y_grp = y_grp_next
-                if c + 1 < N_CHUNKS:
-                    y_grp_next = transpose_y(c + 1)
-                rows = slice(c * CHUNK, (c + 1) * CHUNK)
-                nc.vector.quantize_mx(out=y_codes[:, rows].bitcast(FP8X4), scales=y_scales[:, rows], in_=y_grp[:])
+        def softplus_exp(c):
+            nc.scalar.activation(out=sig_t[:, c, :, :], in_=sig_t[:, c, :, :], func=ACT.Exp)
 
-                sig_sums = d_layout_sums(psum_a, c, H)
-                for h in range(H):
-                    nc.vector.tensor_scalar(
-                        out=sig_t[:, c, h, :],
-                        in0=sig_sums[h][:],
-                        scalar1=par[:, h, ROW_BE_SIG : ROW_BE_SIG + 1],
-                        scalar2=SOFTPLUS_LINEAR_FROM,
-                        op0=ALU.add,
-                        op1=ALU.min,
-                    )
-                nc.scalar.activation(out=sig_t[:, c, :, :], in_=sig_t[:, c, :, :], func=ACT.Exp)
+        def softplus_log(c):
+            nc.scalar.activation(out=sig_t[:, c, :, :], in_=sig_t[:, c, :, :], func=ACT.Ln, bias=one[:])
 
-                mu_out = stage.tile([P, TPC, D], F32, name="mu_out")
-                for pair in range(TPC // 2):
-                    mu_n = psum_a.tile([P, 2, D], F32, name="mu_n")
-                    for i in range(2):
-                        cols = slice(c * CHUNK + (2 * pair + i) * P, c * CHUNK + (2 * pair + i + 1) * P)
-                        nc.tensor.matmul_mx(
-                            out=mu_n[:, i, :],
-                            lhsT=y_codes[:, cols].bitcast(FP8X4),
-                            lhsT_scale=y_scales[:, cols],
-                            rhs=w_codes[:, 0:D].bitcast(FP8X4),
-                            rhs_scale=w_scales[:, 0:D],
-                            start=True,
-                            stop=True,
-                        )
-                    nc.vector.tensor_tensor(
-                        out=mu_out[:, 2 * pair : 2 * pair + 2, :],
-                        in0=mu_n[:],
-                        in1=be_mu_rows[:].unsqueeze(1).to_broadcast([P, 2, D]),
-                        op=ALU.add,
-                    )
-                nc.sync.dma_start(out=mu_view[:, c * TPC : (c + 1) * TPC, :], in_=mu_out[:])
+        def softplus_max(c):
+            sig_sums = d_layout_sums(c, H)
+            for h in range(H):
+                nc.vector.scalar_tensor_tensor(
+                    out=sig_t[:, c, h, :],
+                    in0=sig_sums[h][:],
+                    scalar=par[:, h, ROW_BE_SIG : ROW_BE_SIG + 1],
+                    in1=sig_t[:, c, h, :],
+                    op0=ALU.add,
+                    op1=ALU.max,
+                )
 
-        log_pool = ctx.enter_context(tc.tile_pool(name="logs", bufs=KC + 2))
-        sum_pool = ctx.enter_context(tc.tile_pool(name="log_sums", bufs=SUM_LEAD + 3))
-        wgt_pool = ctx.enter_context(tc.tile_pool(name="wgts", bufs=12))
-        out_pool = ctx.enter_context(tc.tile_pool(name="outs", bufs=2))
-        psum = ctx.enter_context(tc.psum_pool(name="psum", bufs=4))
-
-        for c in range(N_CHUNKS + 1):
-            if c < N_CHUNKS:
-                nc.scalar.activation(out=sig_t[:, c, :, :], in_=sig_t[:, c, :, :], func=ACT.Ln, bias=one[:])
-                sig_sums = d_layout_sums(psum, c, H)
-                for h in range(H):
-                    nc.vector.scalar_tensor_tensor(
-                        out=sig_t[:, c, h, :],
-                        in0=sig_sums[h][:],
-                        scalar=par[:, h, ROW_BE_SIG : ROW_BE_SIG + 1],
-                        in1=sig_t[:, c, h, :],
-                        op0=ALU.add,
-                        op1=ALU.max,
-                    )
-            if c > 0:
-                b = c - 1
-                sig_out = out_pool.tile([P, TPC, D], F32, name="sig_out")
-                for pair in range(TPC // 2):
-                    sig_n = psum.tile([P, 2, D], F32, name="sig_n", tag="acc")
-                    for i in range(2):
-                        cols = slice((2 * pair + i) * P, (2 * pair + i + 1) * P)
-                        for h in range(H):
-                            nc.tensor.transpose(sig_n[:, i, h * P : (h + 1) * P], sig_t[:, b, h, cols], ident[:])
-                    nc.vector.tensor_scalar(
-                        out=sig_out[:, 2 * pair : 2 * pair + 2, :],
-                        in0=sig_n[:],
-                        scalar1=SIG_FLOOR,
-                        scalar2=None,
-                        op0=ALU.add,
-                    )
-                nc.sync.dma_start(out=sig_view[:, b * TPC : (b + 1) * TPC, :], in_=sig_out[:])
+        def store_enc_sig(c):
+            sig_out = out_pool.tile([P, TPC, D], F32, name="sig_out", tag="rows_out")
+            for pair in range(TPC // 2):
+                sig_n = psum.tile([P, 2, D], F32, name="sig_n", tag="acc")
+                for i in range(2):
+                    cols = slice((2 * pair + i) * P, (2 * pair + i + 1) * P)
+                    for h in range(H):
+                        nc.tensor.transpose(sig_n[:, i, h * P : (h + 1) * P], sig_t[:, c, h, cols], ident[:])
+                nc.vector.tensor_scalar(
+                    out=sig_out[:, 2 * pair : 2 * pair + 2, :],
+                    in0=sig_n[:],
+                    scalar1=SIG_FLOOR,
+                    scalar2=None,
+                    op0=ALU.add,
+                )
+            nc.sync.dma_start(out=sig_view[:, c * TPC : (c + 1) * TPC, :], in_=sig_out[:])
 
         logs = {}
         wgts = {}
@@ -261,8 +268,12 @@ def tile_deepgmm_pa_t_kernel(
         accs = {}
         mu_sums = {}
 
-        def gpsimd_squares(j):
-            return j % GPSIMD_EVERY == GPSIMD_EVERY - 1
+        def squarer(j):
+            if j % GPSIMD_EVERY == GPSIMD_EVERY - 1:
+                return "gpsimd"
+            if j >= N_UNITS - KC:
+                return "scalar"
+            return "vector"
 
         def take_logs(c):
             for k in range(KC):
@@ -275,11 +286,11 @@ def tile_deepgmm_pa_t_kernel(
 
         def take_weights(c):
             for j in range(c * KC, (c + 1) * KC):
-                wgt = wgt_pool.tile([P, H, CHUNK], F32, name="wgt")
-                if gpsimd_squares(j):
-                    nc.scalar.activation(out=wgt[:], in_=logs[j][:], func=ACT.Exp, bias=half_ln_half[:], scale=-1.0)
-                else:
+                wgt = big_pool.tile([P, H, CHUNK], F32, name="wgt", tag="big", align_bytes=64)
+                if squarer(j) == "vector":
                     nc.scalar.activation(out=wgt[:], in_=logs[j][:], func=ACT.Exp, bias=ln_half[:], scale=-2.0)
+                else:
+                    nc.scalar.activation(out=wgt[:], in_=logs[j][:], func=ACT.Exp, bias=half_ln_half[:], scale=-1.0)
                 wgts[j] = wgt
 
         def add_logs(j):
@@ -290,7 +301,7 @@ def tile_deepgmm_pa_t_kernel(
         def weighted_squares(j):
             c, k = divmod(j, KC)
             wgt = wgts[j]
-            for step in range(1 if gpsimd_squares(j) else 2):
+            for step in range(2 if squarer(j) == "vector" else 1):
                 for h in range(H):
                     nc.vector.scalar_tensor_tensor(
                         out=wgt[:, h, :],
@@ -300,8 +311,10 @@ def tile_deepgmm_pa_t_kernel(
                         op0=ALU.subtract,
                         op1=ALU.mult,
                     )
-            if gpsimd_squares(j):
+            if squarer(j) == "gpsimd":
                 nc.gpsimd.tensor_tensor(out=wgt[:], in0=wgt[:], in1=wgt[:], op=ALU.mult)
+            if squarer(j) == "scalar":
+                nc.scalar.activation(out=wgt[:], in_=wgt[:], func=ACT.Square)
 
         def add_over_halves(j):
             acc = psum.tile([P, TPC, P], F32, name="acc", tag="acc")
@@ -319,35 +332,61 @@ def tile_deepgmm_pa_t_kernel(
                     )
             accs[j] = acc
 
-        def reduce_unit(j):
-            c, k = divmod(j, KC)
-            nc.vector.tensor_reduce(out=energy[:, k, c * TPC : (c + 1) * TPC], in_=accs[j][:], axis=AX.X, op=ALU.add)
+        def reduce_units(first, end):
+            for j in range(first, end):
+                c, k = divmod(j, KC)
+                nc.vector.tensor_reduce(
+                    out=energy[:, k, c * TPC : (c + 1) * TPC], in_=accs[j][:], axis=AX.X, op=ALU.add
+                )
 
-        mu_sums[0] = d_layout_sums(psum, 0, 0)
+        prepare(0)
+        softplus_exp(0)
+        softplus_log(0)
+        nc.scalar.activation(out=ln_half[:], in_=half[:], func=ACT.Ln)
+        prepare(1)
+        softplus_max(0)
         take_logs(0)
+        for c in range(2, N_CHUNKS):
+            prepare(c)
+        store_enc_sig(0)
+        nc.vector.tensor_scalar(out=half_ln_half[:], in0=ln_half[:], scalar1=0.5, scalar2=None, op0=ALU.mult)
+        mu_sums[0] = d_layout_sums(0, 0)
         take_weights(0)
+        for c in range(1, N_CHUNKS):
+            softplus_exp(c)
         for j in range(SUM_LEAD):
             add_logs(j)
+
+        reduced = 0
         for c in range(N_CHUNKS):
-            if c + 1 < N_CHUNKS:
-                mu_sums[c + 1] = d_layout_sums(psum, c + 1, 0)
-                take_logs(c + 1)
             for j in range(c * KC, (c + 1) * KC):
+                if j == c * KC + NEXT_CHUNK_AT and c + 1 < N_CHUNKS:
+                    if c == 0:
+                        reduce_units(reduced, j)
+                        reduced = j
+                        for b in range(1, N_CHUNKS + 1):
+                            if b < N_CHUNKS:
+                                softplus_log(b)
+                                softplus_max(b)
+                            if b > 1:
+                                store_enc_sig(b - 1)
+                    mu_sums[c + 1] = d_layout_sums(c + 1, 0)
+                    take_logs(c + 1)
                 if j + SUM_LEAD < N_UNITS:
                     add_logs(j + SUM_LEAD)
                 weighted_squares(j)
                 add_over_halves(j)
-                if j >= REDUCE_LAG:
-                    reduce_unit(j - REDUCE_LAG)
+                if j - REDUCE_LAG >= reduced:
+                    reduce_units(reduced, j - REDUCE_LAG + 1)
+                    reduced = j - REDUCE_LAG + 1
             if c + 1 < N_CHUNKS:
                 take_weights(c + 1)
-        for j in range(N_UNITS - REDUCE_LAG, N_UNITS):
-            reduce_unit(j)
+        reduce_units(reduced, N_UNITS)
 
-        z = out_pool.tile([P, N_TILES, KC], F32, name="z")
-        z_max = out_pool.tile([P, N_TILES], F32, name="z_max")
-        z_exp = out_pool.tile([P, N_TILES, KC], F32, name="z_exp")
-        z_sum = out_pool.tile([P, N_TILES], F32, name="z_sum")
+        z = keep.tile([P, N_TILES, KC], F32, name="z")
+        z_max = keep.tile([P, N_TILES], F32, name="z_max")
+        z_exp = keep.tile([P, N_TILES, KC], F32, name="z_exp")
+        z_sum = keep.tile([P, N_TILES], F32, name="z_sum")
         nc.vector.tensor_tensor(
             out=z[:],
             in0=logit_rows[:].unsqueeze(1).to_broadcast([P, N_TILES, KC]),

@@ -37,6 +37,7 @@ GPSIMD_EVERY = 3
 SUM_LEAD = 3
 REDUCE_LAG = 3
 NEXT_CHUNK_AT = 10
+SCALAR_FROM = 4
 BIG_SLOTS = KC
 
 FLOPS = 2 * N_ROWS * K_IN * 2 * D
@@ -271,7 +272,7 @@ def tile_deepgmm_pa_t_kernel(
         def squarer(j):
             if j % GPSIMD_EVERY == GPSIMD_EVERY - 1:
                 return "gpsimd"
-            if j >= N_UNITS - KC:
+            if j >= N_UNITS - KC + SCALAR_FROM:
                 return "scalar"
             return "vector"
 

from contextlib import ExitStack

import concourse.mybir as mybir
from concourse.masks import make_identity

F32 = mybir.dt.float32
BF16 = mybir.dt.bfloat16
U32 = mybir.dt.uint32
U8 = mybir.dt.uint8
FP8X4 = mybir.dt.float8_e4m3fn_x4
ALU = mybir.AluOpType
ACT = mybir.ActivationFunctionType
AX = mybir.AxisListType

P = 128
N_ROWS = 4096
K_IN = 512
D = 256
H = D // P
KC = 16
CHUNK = 512
TPC = CHUNK // P
N_CHUNKS = N_ROWS // CHUNK
N_TILES = N_ROWS // P
N_UNITS = N_CHUNKS * KC
PACK = 4

SIG_FLOOR = 0.001
SOFTPLUS_LINEAR_FROM = 40.0

ROW_PHI_MUS = 0
ROW_PHI_SIGS = KC
ROW_BE_MU = 2 * KC
ROW_BE_SIG = 2 * KC + 1

GPSIMD_EVERY = 3
SUM_LEAD = 3
REDUCE_LAG = 3
NEXT_CHUNK_AT = 10
SCALAR_FROM = 4
BIG_SLOTS = KC

FLOPS = 2 * N_ROWS * K_IN * 2 * D


def tile_deepgmm_pa_t_kernel(
    tc, Y, We_mu, be_mu, We_sig, be_sig, phi_mus, phi_sigs, phi_logits, out_0, out_1, out_2
):
    nc = tc.nc
    y_view = Y.rearrange("(p t) k -> p (t k)", t=N_TILES)
    mu_view = out_0.rearrange("(p t) d -> p t d", t=N_TILES)
    sig_view = out_1.rearrange("(p t) d -> p t d", t=N_TILES)
    z_view = out_2.rearrange("(p t) k -> p (t k)", t=N_TILES)

    with ExitStack() as ctx:
        ctx.enter_context(tc.manual_schedule())
        keep = ctx.enter_context(tc.tile_pool(name="keep", bufs=1))

        ident = keep.tile([P, P], F32, name="ident")
        w_codes = keep.tile([P, 2 * D], U32, name="w_codes", align_bytes=64)
        w_scales = keep.tile([P, 2 * D], U8, name="w_scales", align_bytes=64)
        y_codes = keep.tile([P, N_ROWS], U32, name="y_codes", align_bytes=64)
        y_scales = keep.tile([P, N_ROWS], U8, name="y_scales", align_bytes=64)
        par = keep.tile([P, H, P], F32, name="par")
        mu_shift = keep.tile([P, H, KC], F32, name="mu_shift")
        sig_shift = keep.tile([P, H, KC], F32, name="sig_shift")
        be_mu_rows = keep.tile([P, D], F32, name="be_mu_rows")
        logit_rows = keep.tile([P, KC], F32, name="logit_rows")
        one = keep.tile([P, 1], F32, name="one")
        half = keep.tile([P, 1], F32, name="half")
        ln_half = keep.tile([P, 1], F32, name="ln_half")
        half_ln_half = keep.tile([P, 1], F32, name="half_ln_half")
        sig_t = keep.tile([P, N_CHUNKS, H, CHUNK], F32, name="sig_t")
        energy = keep.tile([P, KC, N_TILES], F32, name="energy")

        log_pool = ctx.enter_context(tc.tile_pool(name="logs", bufs=KC + 2))
        sum_pool = ctx.enter_context(tc.tile_pool(name="log_sums", bufs=SUM_LEAD + 3))
        big_pool = ctx.enter_context(tc.tile_pool(name="big", bufs=BIG_SLOTS))
        out_pool = ctx.enter_context(tc.tile_pool(name="outs", bufs=3))
        psum = ctx.enter_context(tc.psum_pool(name="psum", bufs=4))

        def d_layout_sums(c, first_block):
            rows = slice(c * CHUNK, (c + 1) * CHUNK)
            sums = []
            for h in range(H):
                cols = slice((first_block + h) * P, (first_block + h + 1) * P)
                d_sum = psum.tile([P, CHUNK], F32, name="d_sum", tag="d_sum")
                nc.tensor.matmul_mx(
                    out=d_sum[:],
                    lhsT=w_codes[:, cols].bitcast(FP8X4),
                    lhsT_scale=w_scales[:, cols],
                    rhs=y_codes[:, rows].bitcast(FP8X4),
                    rhs_scale=y_scales[:, rows],
                    start=True,
                    stop=True,
                )
                sums.append(d_sum)
            return sums

        make_identity(nc, ident[:])

        rows_bf = keep.tile([P, D], BF16, name="rows_bf")
        nc.vector.memset(rows_bf[:], 0.0)
        nc.scalar.dma_start(out=rows_bf[ROW_PHI_MUS : ROW_PHI_MUS + KC, :], in_=phi_mus)
        nc.scalar.dma_start(out=rows_bf[ROW_PHI_SIGS : ROW_PHI_SIGS + KC, :], in_=phi_sigs)
        nc.scalar.dma_start(out=rows_bf[ROW_BE_MU : ROW_BE_MU + 1, :], in_=be_mu.rearrange("(o d) -> o d", o=1))
        nc.scalar.dma_start(out=rows_bf[ROW_BE_SIG : ROW_BE_SIG + 1, :], in_=be_sig.rearrange("(o d) -> o d", o=1))
        be_mu_bf = keep.tile([P, D], BF16, name="be_mu_bf")
        nc.scalar.dma_start(out=be_mu_bf[:], in_=be_mu.partition_broadcast(P))
        logit_bf = keep.tile([P, KC], BF16, name="logit_bf")
        nc.scalar.dma_start(out=logit_bf[:], in_=phi_logits.partition_broadcast(P))
        nc.vector.memset(one[:], 1.0)
        nc.vector.memset(half[:], 0.5)

        y_raw = []
        w_raw = big_pool.tile([P, PACK, 2 * D], BF16, name="w_raw", tag="big", align_bytes=64)
        for c in range(N_CHUNKS):
            y_chunk = big_pool.tile([P, TPC * K_IN], BF16, name="y_chunk", tag="big", align_bytes=64)
            nc.sync.dma_start(out=y_chunk[:], in_=y_view[:, c * TPC * K_IN : (c + 1) * TPC * K_IN])
            y_raw.append(y_chunk)
            if c == 0:
                for m, weight in enumerate((We_mu, We_sig)):
                    for u in range(2):
                        nc.sync.dma_start(
                            out=w_raw[:, 2 * u : 2 * u + 2, m * D : (m + 1) * D],
                            in_=weight[u * 2 * P : (u + 1) * 2 * P, :].rearrange("(q e) c -> q e c", e=2),
                        )

        y_banks = {}
        y_grps = {}

        def transpose_y(c):
            words = y_raw[c][:].bitcast(F32)
            y_banks[c] = []
            for pair in range(TPC // 2):
                y_t = psum.tile([P, 2, 2 * P], F32, name="y_t", tag="acc")
                for i in range(2):
                    first_word = (2 * pair + i) * (K_IN // 2)
                    for u in range(2):
                        nc.tensor.transpose(
                            y_t[:, u, i * P : (i + 1) * P],
                            words[:, first_word + u * P : first_word + (u + 1) * P],
                            ident[:],
                        )
                y_banks[c].append(y_t)

        def regroup_y(c):
            y_grp = big_pool.tile([P, PACK * CHUNK], BF16, name="y_grp", tag="big", align_bytes=64)
            grp_words = y_grp[:].bitcast(F32)
            for pair in range(TPC // 2):
                nc.vector.tensor_copy(
                    out=grp_words[:, pair * 4 * P : (pair + 1) * 4 * P].rearrange("p (n u) -> p n u", u=2),
                    in_=y_banks[c][pair][:].rearrange("p u n -> p n u"),
                )
            y_grps[c] = y_grp

        transpose_y(0)
        regroup_y(0)

        w_grp = big_pool.tile([P, 2 * D, PACK], BF16, name="w_grp", tag="big", align_bytes=64)
        nc.vector.tensor_copy(out=w_grp[:], in_=w_raw[:].rearrange("p t c -> p c t"))
        rows_f32 = keep.tile([P, D], F32, name="rows_f32")
        nc.vector.tensor_copy(out=rows_f32[:], in_=rows_bf[:])
        nc.vector.quantize_mx(
            out=w_codes[:].bitcast(FP8X4), scales=w_scales[:], in_=w_grp[:].rearrange("p c t -> p (c t)")
        )
        par_ps = psum.tile([P, H, P], F32, name="par_ps", tag="acc")
        for h in range(H):
            nc.tensor.transpose(par_ps[:, h, :], rows_f32[:, h * P : (h + 1) * P], ident[:])
        nc.vector.tensor_copy(out=par[:], in_=par_ps[:])
        nc.vector.tensor_copy(out=be_mu_rows[:], in_=be_mu_bf[:])
        nc.vector.tensor_copy(out=logit_rows[:], in_=logit_bf[:])
        for h in range(H):
            nc.vector.tensor_scalar(
                out=mu_shift[:, h, :],
                in0=par[:, h, ROW_PHI_MUS : ROW_PHI_MUS + KC],
                scalar1=par[:, h, ROW_BE_MU : ROW_BE_MU + 1],
                scalar2=None,
                op0=ALU.subtract,
            )
        nc.vector.tensor_scalar(
            out=sig_shift[:],
            in0=par[:, :, ROW_PHI_SIGS : ROW_PHI_SIGS + KC],
            scalar1=SIG_FLOOR,
            scalar2=None,
            op0=ALU.add,
        )

        def prepare(c):
            if c + 1 < N_CHUNKS:
                transpose_y(c + 1)
            rows = slice(c * CHUNK, (c + 1) * CHUNK)
            nc.vector.quantize_mx(out=y_codes[:, rows].bitcast(FP8X4), scales=y_scales[:, rows], in_=y_grps[c][:])
            sig_sums = d_layout_sums(c, H)
            mu_banks = []
            for pair in range(TPC // 2):
                mu_n = psum.tile([P, 2, D], F32, name="mu_n", tag="acc")
                for i in range(2):
                    cols = slice(c * CHUNK + (2 * pair + i) * P, c * CHUNK + (2 * pair + i + 1) * P)
                    nc.tensor.matmul_mx(
                        out=mu_n[:, i, :],
                        lhsT=y_codes[:, cols].bitcast(FP8X4),
                        lhsT_scale=y_scales[:, cols],
                        rhs=w_codes[:, 0:D].bitcast(FP8X4),
                        rhs_scale=w_scales[:, 0:D],
                        start=True,
                        stop=True,
                    )
                mu_banks.append(mu_n)
            if c + 1 < N_CHUNKS:
                regroup_y(c + 1)
            for h in range(H):
                nc.vector.tensor_scalar(
                    out=sig_t[:, c, h, :],
                    in0=sig_sums[h][:],
                    scalar1=par[:, h, ROW_BE_SIG : ROW_BE_SIG + 1],
                    scalar2=SOFTPLUS_LINEAR_FROM,
                    op0=ALU.add,
                    op1=ALU.min,
                )
            mu_out = out_pool.tile([P, TPC, D], F32, name="mu_out", tag="rows_out")
            for pair in range(TPC // 2):
                nc.vector.tensor_tensor(
                    out=mu_out[:, 2 * pair : 2 * pair + 2, :],
                    in0=mu_banks[pair][:],
                    in1=be_mu_rows[:].unsqueeze(1).to_broadcast([P, 2, D]),
                    op=ALU.add,
                )
            nc.sync.dma_start(out=mu_view[:, c * TPC : (c + 1) * TPC, :], in_=mu_out[:])

        def softplus_exp(c):
            nc.scalar.activation(out=sig_t[:, c, :, :], in_=sig_t[:, c, :, :], func=ACT.Exp)

        def softplus_log(c):
            nc.scalar.activation(out=sig_t[:, c, :, :], in_=sig_t[:, c, :, :], func=ACT.Ln, bias=one[:])

        def softplus_max(c):
            sig_sums = d_layout_sums(c, H)
            for h in range(H):
                nc.vector.scalar_tensor_tensor(
                    out=sig_t[:, c, h, :],
                    in0=sig_sums[h][:],
                    scalar=par[:, h, ROW_BE_SIG : ROW_BE_SIG + 1],
                    in1=sig_t[:, c, h, :],
                    op0=ALU.add,
                    op1=ALU.max,
                )

        def store_enc_sig(c):
            sig_out = out_pool.tile([P, TPC, D], F32, name="sig_out", tag="rows_out")
            for pair in range(TPC // 2):
                sig_n = psum.tile([P, 2, D], F32, name="sig_n", tag="acc")
                for i in range(2):
                    cols = slice((2 * pair + i) * P, (2 * pair + i + 1) * P)
                    for h in range(H):
                        nc.tensor.transpose(sig_n[:, i, h * P : (h + 1) * P], sig_t[:, c, h, cols], ident[:])
                nc.vector.tensor_scalar(
                    out=sig_out[:, 2 * pair : 2 * pair + 2, :],
                    in0=sig_n[:],
                    scalar1=SIG_FLOOR,
                    scalar2=None,
                    op0=ALU.add,
                )
            nc.sync.dma_start(out=sig_view[:, c * TPC : (c + 1) * TPC, :], in_=sig_out[:])

        logs = {}
        wgts = {}
        log_sums = {}
        accs = {}
        mu_sums = {}

        def squarer(j):
            if j % GPSIMD_EVERY == GPSIMD_EVERY - 1:
                return "gpsimd"
            if j >= N_UNITS - KC + SCALAR_FROM:
                return "scalar"
            return "vector"

        def take_logs(c):
            for k in range(KC):
                unit_logs = log_pool.tile([P, H, CHUNK], F32, name="unit_logs")
                for h in range(H):
                    nc.scalar.activation(
                        out=unit_logs[:, h, :], in_=sig_t[:, c, h, :], func=ACT.Ln, bias=sig_shift[:, h, k : k + 1]
                    )
                logs[c * KC + k] = unit_logs

        def take_weights(c):
            for j in range(c * KC, (c + 1) * KC):
                wgt = big_pool.tile([P, H, CHUNK], F32, name="wgt", tag="big", align_bytes=64)
                if squarer(j) == "vector":
                    nc.scalar.activation(out=wgt[:], in_=logs[j][:], func=ACT.Exp, bias=ln_half[:], scale=-2.0)
                else:
                    nc.scalar.activation(out=wgt[:], in_=logs[j][:], func=ACT.Exp, bias=half_ln_half[:], scale=-1.0)
                wgts[j] = wgt

        def add_logs(j):
            log_sum = sum_pool.tile([P, CHUNK], F32, name="log_sum")
            nc.gpsimd.tensor_tensor(out=log_sum[:], in0=logs[j][:, 0, :], in1=logs[j][:, 1, :], op=ALU.add)
            log_sums[j] = log_sum

        def weighted_squares(j):
            c, k = divmod(j, KC)
            wgt = wgts[j]
            for step in range(2 if squarer(j) == "vector" else 1):
                for h in range(H):
                    nc.vector.scalar_tensor_tensor(
                        out=wgt[:, h, :],
                        in0=mu_sums[c][h][:],
                        scalar=mu_shift[:, h, k : k + 1],
                        in1=wgt[:, h, :],
                        op0=ALU.subtract,
                        op1=ALU.mult,
                    )
            if squarer(j) == "gpsimd":
                nc.gpsimd.tensor_tensor(out=wgt[:], in0=wgt[:], in1=wgt[:], op=ALU.mult)
            if squarer(j) == "scalar":
                nc.scalar.activation(out=wgt[:], in_=wgt[:], func=ACT.Square)

        def add_over_halves(j):
            acc = psum.tile([P, TPC, P], F32, name="acc", tag="acc")
            for t in range(TPC):
                cols = slice(t * P, (t + 1) * P)
                parts = (log_sums[j][:, cols], wgts[j][:, 0, cols], wgts[j][:, 1, cols])
                for i, part in enumerate(parts):
                    nc.tensor.matmul(
                        out=acc[:, t, :],
                        lhsT=part,
                        rhs=ident[:],
                        is_transpose=True,
                        start=(i == 0),
                        stop=(i == len(parts) - 1),
                    )
            accs[j] = acc

        def reduce_units(first, end):
            for j in range(first, end):
                c, k = divmod(j, KC)
                nc.vector.tensor_reduce(
                    out=energy[:, k, c * TPC : (c + 1) * TPC], in_=accs[j][:], axis=AX.X, op=ALU.add
                )

        prepare(0)
        softplus_exp(0)
        softplus_log(0)
        nc.scalar.activation(out=ln_half[:], in_=half[:], func=ACT.Ln)
        prepare(1)
        softplus_max(0)
        take_logs(0)
        for c in range(2, N_CHUNKS):
            prepare(c)
        store_enc_sig(0)
        nc.vector.tensor_scalar(out=half_ln_half[:], in0=ln_half[:], scalar1=0.5, scalar2=None, op0=ALU.mult)
        mu_sums[0] = d_layout_sums(0, 0)
        take_weights(0)
        for c in range(1, N_CHUNKS):
            softplus_exp(c)
        for j in range(SUM_LEAD):
            add_logs(j)

        reduced = 0
        for c in range(N_CHUNKS):
            for j in range(c * KC, (c + 1) * KC):
                if j == c * KC + NEXT_CHUNK_AT and c + 1 < N_CHUNKS:
                    if c == 0:
                        reduce_units(reduced, j)
                        reduced = j
                        for b in range(1, N_CHUNKS + 1):
                            if b < N_CHUNKS:
                                softplus_log(b)
                                softplus_max(b)
                            if b > 1:
                                store_enc_sig(b - 1)
                    mu_sums[c + 1] = d_layout_sums(c + 1, 0)
                    take_logs(c + 1)
                if j + SUM_LEAD < N_UNITS:
                    add_logs(j + SUM_LEAD)
                weighted_squares(j)
                add_over_halves(j)
                if j - REDUCE_LAG >= reduced:
                    reduce_units(reduced, j - REDUCE_LAG + 1)
                    reduced = j - REDUCE_LAG + 1
            if c + 1 < N_CHUNKS:
                take_weights(c + 1)
        reduce_units(reduced, N_UNITS)

        z = keep.tile([P, N_TILES, KC], F32, name="z")
        z_max = keep.tile([P, N_TILES], F32, name="z_max")
        z_exp = keep.tile([P, N_TILES, KC], F32, name="z_exp")
        z_sum = keep.tile([P, N_TILES], F32, name="z_sum")
        nc.vector.tensor_tensor(
            out=z[:],
            in0=logit_rows[:].unsqueeze(1).to_broadcast([P, N_TILES, KC]),
            in1=energy[:].rearrange("p k t -> p t k"),
            op=ALU.subtract,
        )
        nc.vector.tensor_reduce(out=z_max[:], in_=z[:], axis=AX.X, op=ALU.max)
        nc.vector.tensor_tensor(
            out=z[:], in0=z[:], in1=z_max[:].unsqueeze(2).to_broadcast([P, N_TILES, KC]), op=ALU.subtract
        )
        nc.scalar.activation(out=z_exp[:], in_=z[:], func=ACT.Exp)
        nc.vector.tensor_reduce(out=z_sum[:], in_=z_exp[:], axis=AX.X, op=ALU.add)
        nc.scalar.activation(out=z_sum[:], in_=z_sum[:], func=ACT.Ln)
        nc.vector.tensor_tensor(
            out=z[:], in0=z[:], in1=z_sum[:].unsqueeze(2).to_broadcast([P, N_TILES, KC]), op=ALU.subtract
        )
        nc.sync.dma_start(out=z_view, in_=z[:].rearrange("p t k -> p (t k)"))
